import numpy as np
import ml_dtypes


def mxq(x, axis, fmt="e4m3"):
    dtype, down = {"e4m3": (ml_dtypes.float8_e4m3fn, 7), "e5m2": (ml_dtypes.float8_e5m2, 14)}[fmt]
    v = np.moveaxis(np.asarray(x, np.float32).astype(ml_dtypes.bfloat16).astype(np.float64), axis, -1)
    blocks = v.reshape(v.shape[:-1] + (-1, 32))
    amax = np.abs(blocks).max(-1, keepdims=True)
    byte = np.maximum(np.where(amax > 0, np.frexp(amax)[1] - 1 + 127, 0) - down, 1)
    scale = np.exp2(byte - 127.0)
    codes = (blocks / scale).astype(np.float32).astype(dtype).astype(np.float64)
    return np.moveaxis((codes * scale).reshape(v.shape), -1, axis)


BF16 = ml_dtypes.bfloat16


def bf(x):
    return np.asarray(x, np.float32).astype(BF16)


def f64(x):
    return np.asarray(x).astype(np.float64)


B, C, H, W = 1, 128, 64, 64
N = H * W
A = np.sqrt(3.0 / np.sqrt(C))


def sigmoid(v):
    return 1.0 / (1.0 + np.exp(-v))


def setup_inputs():
    q = np.random.standard_normal((B, C, H, W)) * A
    s = np.random.standard_normal((B, C, H, W)) * A
    s = s - s.mean(axis=(2, 3), keepdims=True) + np.random.standard_normal((B, C, 1, 1)) * 1.5 / (A * np.sqrt(C) * N)
    return {"query_feature": bf(q), "support_feature": bf(s)}


def reference(query_feature, support_feature):
    q, s = f64(query_feature), f64(support_feature)
    qf = q.reshape(B, N, C)
    sf = s.reshape(B, C, N)
    adj = qf @ sf
    e = np.exp(adj - adj.max(-1, keepdims=True))
    logits = (mxq(e, 2, "e4m3") @ mxq(qf, 1, "e4m3")) / e.sum(-1, keepdims=True)
    gate = sigmoid(adj.sum(-1))
    logits = logits * gate[..., None]
    sup = s.reshape(B, N, C) * gate[..., None]
    return (q + logits.reshape(B, C, H, W), s + sup.reshape(B, C, H, W))

@@ -1,0 +1,266 @@
+from contextlib import ExitStack
+
+import concourse.bass as bass
+import concourse.mybir as mybir
+import concourse.tile as tile
+from concourse.masks import make_identity
+
+F32 = mybir.dt.float32
+BF16 = mybir.dt.bfloat16
+U32 = mybir.dt.uint32
+U8 = mybir.dt.uint8
+FP8X4 = mybir.dt.float8_e4m3fn_x4
+ALU = mybir.AluOpType
+ACTF = mybir.ActivationFunctionType
+AX = mybir.AxisListType
+
+P = 128
+N = 4096
+C = 128
+NB = N // P
+G = N // 512
+FLOPS = 2 * 2 * N * N * C
+
+MANUAL = True
+POLICY = [("A", True), ("A", True), ("A", True), ("A", True)]
+
+
+def tile_fusionfeature_layer_kernel(tc, query_feature, support_feature, out_0, out_1):
+    nc = tc.nc
+    q_d = query_feature.rearrange("o c h w -> (o c) (h w)")
+    s_d = support_feature.rearrange("o c h w -> (o c) (h w)")
+    qmx_d = query_feature.rearrange("o (g a) (b h) w -> (o a b) g (h w)", g=G, a=16, b=8)
+    o0_d = out_0.rearrange("o c h w -> (o c) (h w)")
+    o1_d = out_1.rearrange("o c h w -> (o c) (h w)")
+
+    with ExitStack() as ctx:
+        const = ctx.enter_context(tc.tile_pool(name="const", bufs=1))
+        work = ctx.enter_context(tc.tile_pool(name="work", bufs=2))
+        psum = ctx.enter_context(tc.psum_pool(name="psum", bufs=2))
+        if MANUAL:
+            ctx.enter_context(tc.manual_schedule())
+
+        ident = const.tile([P, P], BF16, name="ident")
+        make_identity(nc, ident[:])
+
+        q_nat = const.tile([P, N], BF16, name="q_nat")
+        s_nat = const.tile([P, N], BF16, name="s_nat")
+        qmx_raw = const.tile([P, G, 512], BF16, name="qmx_raw")
+        def load(dst, src, ch):
+            cols = slice(ch * 1024, (ch + 1) * 1024)
+            nc.sync.dma_start(out=dst[:, cols], in_=src[:, cols])
+
+        load(q_nat, q_d, 0)
+        for ch in range(4):
+            load(s_nat, s_d, ch)
+        nc.sync.dma_start(out=qmx_raw[:], in_=qmx_d)
+        for ch in range(1, 4):
+            load(q_nat, q_d, ch)
+
+        qfT = const.tile([P, N], BF16, name="qfT")
+
+        def qft_bank(kb):
+            tq = psum.tile([P, 1024], BF16, name="tq", tag="tp", bufs=4)
+            for r in range(8):
+                b = kb * 8 + r
+                nc.tensor.transpose(tq[:, r * P:(r + 1) * P], q_nat[:, b * P:(b + 1) * P], ident[:])
+            if kb == 0:
+                nc.vector.tensor_copy(out=qfT[:, kb * 1024:(kb + 1) * 1024], in_=tq[:])
+            else:
+                nc.scalar.copy(out=qfT[:, kb * 1024:(kb + 1) * 1024], in_=tq[:])
+
+        qft_bank(0)
+
+        sfp = const.tile([P, N], BF16, name="sfp")
+        for g in range(G):
+            cols = slice(g * 512, (g + 1) * 512)
+            dst = sfp[:, cols].rearrange("c (t p) -> c t p", t=4)
+            src = s_nat[:, cols].rearrange("c (p t) -> c t p", t=4)
+            if g == 0:
+                nc.vector.tensor_copy(out=dst, in_=src)
+            else:
+                nc.scalar.copy(out=dst, in_=src)
+
+        tree = const.tile([P, 2048], F32, name="tree")
+        nc.gpsimd.tensor_tensor(out=tree[:], in0=s_nat[:, 0:2048], in1=s_nat[:, 2048:4096], op=ALU.add)
+        for wd in (1024, 512, 256, 128, 64):
+            nc.gpsimd.tensor_tensor(out=tree[:, 0:wd], in0=tree[:, 0:wd], in1=tree[:, wd:2 * wd], op=ALU.add)
+
+        qgrp = const.tile([P, N], BF16, name="qgrp", align_bytes=64)
+        nc.gpsimd.tensor_scalar(
+            out=qgrp[:].rearrange("p (g c t) -> p g c t", g=G, t=4),
+            in0=qmx_raw[:].rearrange("p g (t c) -> p g c t", t=4),
+            scalar1=1.0, scalar2=0.0, op0=ALU.mult, op1=ALU.add)
+        qcodes = const.tile([P, G * C], U32, name="qcodes", align_bytes=64)
+        qscl = const.tile([P, G * C], U8, name="qscl", align_bytes=64)
+
+        ssum = const.tile([P, 1], F32, name="ssum")
+        ssp = const.tile([P, 32], BF16, name="ssp")
+        res1 = const.tile([P, 1], F32, name="res1")
+        res2 = const.tile([P, 1], F32, name="res2")
+        vsum = const.tile([P, NB], F32, name="vsum")
+        gexp = const.tile([P, NB], F32, name="gexp")
+        gden = const.tile([P, NB], F32, name="gden")
+        gate = const.tile([P, NB], F32, name="gate")
+        gate1 = const.tile([P, NB], F32, name="gate1")
+        o1 = const.tile([P, N], F32, name="o1")
+        nc.vector.memset(ssp[:], 0.0)
+
+        def gate_split():
+            nc.vector.tensor_reduce(out=ssum[:], in_=tree[:, 0:64], axis=AX.X, op=ALU.add)
+            nc.vector.tensor_copy(out=ssp[:, 0:1], in_=ssum[:])
+            nc.vector.tensor_tensor(out=res1[:], in0=ssum[:], in1=ssp[:, 0:1], op=ALU.subtract)
+            nc.vector.tensor_copy(out=ssp[:, 1:2], in_=res1[:])
+            nc.vector.tensor_tensor(out=res2[:], in0=res1[:], in1=ssp[:, 1:2], op=ALU.subtract)
+            nc.vector.tensor_copy(out=ssp[:, 2:3], in_=res2[:])
+
+        def gate_matmuls():
+            for hb in range(2):
+                gp = psum.tile([P, 512], F32, name="gp", tag="adj", bufs=2)
+                for r in range(16):
+                    b = hb * 16 + r
+                    nc.tensor.matmul(out=gp[:, r * 32:(r + 1) * 32], lhsT=qfT[:, b * P:(b + 1) * P], rhs=ssp[:],
+                                     start=True, stop=True)
+                nc.vector.tensor_reduce(out=vsum[:, hb * 16:(hb + 1) * 16],
+                                        in_=gp[:].rearrange("p (r j) -> p r j", j=32)[:, :, 0:3],
+                                        axis=AX.X, op=ALU.add)
+
+        def gate_exp():
+            nc.scalar.activation(out=gexp[:], in_=vsum[:], func=ACTF.Exp, scale=-1.0)
+
+        def gate_finish():
+            nc.vector.tensor_scalar_add(out=gden[:], in0=gexp[:], scalar1=1.0)
+            nc.vector.reciprocal(out=gate[:], in_=gden[:])
+            nc.vector.tensor_scalar_add(out=gate1[:], in0=gate[:], scalar1=1.0)
+
+        def out1_piece(ch):
+            cols = slice(ch * 1024, (ch + 1) * 1024)
+            nc.vector.tensor_tensor(
+                out=o1[:, cols].rearrange("p (b k) -> p b k", k=P),
+                in0=s_nat[:, cols].rearrange("p (b k) -> p b k", k=P),
+                in1=gate1[:, ch * 8:(ch + 1) * 8].unsqueeze(2).to_broadcast([P, 8, P]),
+                op=ALU.mult)
+            nc.sync.dma_start(out=o1_d[:, cols], in_=o1[:, cols])
+
+        o0 = const.tile([P, N], F32, name="o0")
+        rs = const.tile([P, NB], F32, name="rs")
+        st = {}
+
+        def adj_evac(b, j):
+            if j == 0:
+                st["adjs", b] = work.tile([P, N], F32, name="adjs", tag="adjs", bufs=3)
+                st["mx8", b] = work.tile([P, 8], F32, name="mx8", tag="mx8", bufs=3)
+            ap = psum.tile([P, 512], F32, name="ap", tag="adj", bufs=2)
+            nc.tensor.matmul(out=ap[:], lhsT=qfT[:, b * P:(b + 1) * P], rhs=sfp[:, j * 512:(j + 1) * 512],
+                             start=True, stop=True)
+            nc.vector.tensor_scalar(out=st["adjs", b][:, j * 512:(j + 1) * 512], in0=ap[:], scalar1=1.0,
+                                    scalar2=None, op0=ALU.mult, op1=ALU.max,
+                                    accum_out=st["mx8", b][:, j:j + 1])
+
+        def negmax(b):
+            nm = work.tile([P, 1], F32, name="nm", tag="nm", bufs=3)
+            st["nm", b] = nm
+            nc.vector.tensor_reduce(out=nm[:], in_=st["mx8", b][:], axis=AX.X, op=ALU.max, negate=True)
+
+        def expo(b):
+            e = work.tile([P, N], BF16, name="e", tag="e", bufs=2)
+            st["e", b] = e
+            nc.scalar.activation(out=e[:], in_=st["adjs", b][:], func=ACTF.Exp, bias=st["nm", b][:],
+                                 scale=1.0, accum_out=rs[:, b:b + 1])
+
+        def transp(b, s):
+            k, r = divmod(s, 8)
+            if r == 0:
+                st["tp", b, k] = psum.tile([P, 1024], BF16, name="tp", tag="tp", bufs=4)
+            nc.tensor.transpose(st["tp", b, k][:, r * P:(r + 1) * P], st["e", b][:, s * P:(s + 1) * P], ident[:])
+
+        def copyout(b, k):
+            if k == 0:
+                st["grp", b] = work.tile([P, N], BF16, name="grp", tag="grp", bufs=2, align_bytes=64)
+                st["pl", b] = work.tile([P, N], BF16, name="pl", tag="pl", bufs=2)
+            eng, via = POLICY[k]
+            cols = slice(k * 1024, (k + 1) * 1024)
+            tp = st["tp", b, k]
+            gdst = st["grp", b][:, cols].rearrange("p (g n t) -> p g n t", g=2, t=4)
+            if via:
+                dst = st["pl", b][:, cols]
+                src = tp[:]
+            else:
+                dst = gdst
+                src = tp[:].rearrange("p (g t n) -> p g n t", g=2, t=4)
+            if eng == "A":
+                nc.scalar.copy(out=dst, in_=src)
+            else:
+                nc.vector.tensor_copy(out=dst, in_=src)
+            if via:
+                nc.gpsimd.tensor_scalar(out=gdst,
+                                        in0=st["pl", b][:, cols].rearrange("p (g t n) -> p g n t", g=2, t=4),
+                                        scalar1=1.0, scalar2=0.0, op0=ALU.mult, op1=ALU.add)
+
+        def quant(b):
+            codes = work.tile([P, G * P], U32, name="codes", tag="codes", bufs=2, align_bytes=64)
+            scl = work.tile([P, G * P], U8, name="scl", tag="scl", bufs=2, align_bytes=64)
+            st["codes", b] = codes
+            st["scl", b] = scl
+            nc.vector.quantize_mx(out=codes[:].bitcast(FP8X4), scales=scl[:], in_=st["grp", b][:])
+
+        def mx(b):
+            acc = psum.tile([P, C], F32, name="acc", tag="acc", bufs=2)
+            st["acc", b] = acc
+            for g in range(G):
+                cols = slice(g * P, (g + 1) * P)
+                nc.tensor.matmul_mx(out=acc[:], lhsT=st["codes", b][:, cols].bitcast(FP8X4),
+                                    lhsT_scale=st["scl", b][:, cols],
+                                    rhs=qcodes[:, cols].bitcast(FP8X4), rhs_scale=qscl[:, cols],
+                                    start=(g == 0), stop=(g == G - 1))
+
+        def epi(b):
+            rinv = work.tile([P, 1], F32, name="rinv", tag="rinv", bufs=3)
+            wgt = work.tile([P, 1], F32, name="wgt", tag="wgt", bufs=3)
+            nc.vector.reciprocal(out=rinv[:], in_=rs[:, b:b + 1])
+            nc.vector.tensor_tensor(out=wgt[:], in0=rinv[:], in1=gate[:, b:b + 1], op=ALU.mult)
+            cols = slice(b * P, (b + 1) * P)
+            nc.vector.scalar_tensor_tensor(out=o0[:, cols], in0=st["acc", b][:], scalar=wgt[:], in1=q_nat[:, cols],
+                                           op0=ALU.mult, op1=ALU.add)
+            if b % 4 == 3:
+                cc = slice((b - 3) * P, (b + 1) * P)
+                nc.sync.dma_start(out=o0_d[:, cc], in_=o0[:, cc])
+
+        for i in range(NB + 4):
+            if i == 3:
+                nc.vector.quantize_mx(out=qcodes[:].bitcast(FP8X4), scales=qscl[:], in_=qgrp[:])
+            if 0 <= i - 4 < NB:
+                quant(i - 4)
+            if i == 2:
+                gate_matmuls()
+            if 0 <= i - 1 < NB:
+                expo(i - 1)
+            if i == 2:
+                gate_exp()
+            if i == NB:
+                out1_piece(0)
+            for j in range(8):
+                if i < NB:
+                    adj_evac(i, j)
+                if 0 <= i - 2 < NB:
+                    for s in range(4 * j, 4 * j + 4):
+                        transp(i - 2, s)
+                if j == 5 and 0 <= i - 4 < NB:
+                    mx(i - 4)
+            if i == 0:
+                for kb in range(1, 4):
+                    qft_bank(kb)
+            if i < NB:
+                negmax(i)
+            if i == 1:
+                gate_split()
+            if i == 2:
+                gate_finish()
+            if 0 <= i - 2 < NB:
+                for k in range(4):
+                    copyout(i - 2, k)
+            if 0 <= i - 4 < NB:
+                epi(i - 4)
+            if i == NB:
+                for ch in range(1, 4):
+                    out1_piece(ch)

@@ -22,7 +22,7 @@ G = N // 512
 FLOPS = 2 * 2 * N * N * C
 
 MANUAL = True
-POLICY = [("A", True), ("A", True), ("A", True), ("A", True)]
+POLICY = [("V", True), ("A", False), ("V", True), ("A", False)]
 
 
 def tile_fusionfeature_layer_kernel(tc, query_feature, support_feature, out_0, out_1):

@@ -22,7 +22,7 @@ G = N // 512
 FLOPS = 2 * 2 * N * N * C
 
 MANUAL = True
-POLICY = [("V", True), ("A", False), ("V", True), ("A", False)]
+POLICY = [("V", True), ("A", True), ("A", True), ("A", True)]
 
 
 def tile_fusionfeature_layer_kernel(tc, query_feature, support_feature, out_0, out_1):
@@ -60,7 +60,7 @@ def tile_fusionfeature_layer_kernel(tc, query_feature, support_feature, out_0, o
         qfT = const.tile([P, N], BF16, name="qfT")
 
         def qft_bank(kb):
-            tq = psum.tile([P, 1024], BF16, name="tq", tag="tp", bufs=4)
+            tq = psum.tile([P, 1024], BF16, name="tq", tag="tp", bufs=3)
             for r in range(8):
                 b = kb * 8 + r
                 nc.tensor.transpose(tq[:, r * P:(r + 1) * P], q_nat[:, b * P:(b + 1) * P], ident[:])
@@ -116,7 +116,7 @@ def tile_fusionfeature_layer_kernel(tc, query_feature, support_feature, out_0, o
 
         def gate_matmuls():
             for hb in range(2):
-                gp = psum.tile([P, 512], F32, name="gp", tag="adj", bufs=2)
+                gp = psum.tile([P, 512], F32, name="gp", tag="adj", bufs=4)
                 for r in range(16):
                     b = hb * 16 + r
                     nc.tensor.matmul(out=gp[:, r * 32:(r + 1) * 32], lhsT=qfT[:, b * P:(b + 1) * P], rhs=ssp[:],
@@ -150,7 +150,7 @@ def tile_fusionfeature_layer_kernel(tc, query_feature, support_feature, out_0, o
             if j == 0:
                 st["adjs", b] = work.tile([P, N], F32, name="adjs", tag="adjs", bufs=3)
                 st["mx8", b] = work.tile([P, 8], F32, name="mx8", tag="mx8", bufs=3)
-            ap = psum.tile([P, 512], F32, name="ap", tag="adj", bufs=2)
+            ap = psum.tile([P, 512], F32, name="ap", tag="adj", bufs=4)
             nc.tensor.matmul(out=ap[:], lhsT=qfT[:, b * P:(b + 1) * P], rhs=sfp[:, j * 512:(j + 1) * 512],
                              start=True, stop=True)
             nc.vector.tensor_scalar(out=st["adjs", b][:, j * 512:(j + 1) * 512], in0=ap[:], scalar1=1.0,
@@ -171,7 +171,7 @@ def tile_fusionfeature_layer_kernel(tc, query_feature, support_feature, out_0, o
         def transp(b, s):
             k, r = divmod(s, 8)
             if r == 0:
-                st["tp", b, k] = psum.tile([P, 1024], BF16, name="tp", tag="tp", bufs=4)
+                st["tp", b, k] = psum.tile([P, 1024], BF16, name="tp", tag="tp", bufs=3)
             nc.tensor.transpose(st["tp", b, k][:, r * P:(r + 1) * P], st["e", b][:, s * P:(s + 1) * P], ident[:])
 
         def copyout(b, k):
@@ -205,7 +205,7 @@ def tile_fusionfeature_layer_kernel(tc, query_feature, support_feature, out_0, o
             nc.vector.quantize_mx(out=codes[:].bitcast(FP8X4), scales=scl[:], in_=st["grp", b][:])
 
         def mx(b):
-            acc = psum.tile([P, C], F32, name="acc", tag="acc", bufs=2)
+            acc = psum.tile([P, C], F32, name="acc", tag="acc", bufs=1)
             st["acc", b] = acc
             for g in range(G):
                 cols = slice(g * P, (g + 1) * P)
@@ -226,11 +226,13 @@ def tile_fusionfeature_layer_kernel(tc, query_feature, support_feature, out_0, o
                 cc = slice((b - 3) * P, (b + 1) * P)
                 nc.sync.dma_start(out=o0_d[:, cc], in_=o0[:, cc])
 
-        for i in range(NB + 4):
+        for i in range(NB + 6):
             if i == 3:
                 nc.vector.quantize_mx(out=qcodes[:].bitcast(FP8X4), scales=qscl[:], in_=qgrp[:])
             if 0 <= i - 4 < NB:
                 quant(i - 4)
+            if 0 <= i - 5 < NB:
+                epi(i - 5)
             if i == 2:
                 gate_matmuls()
             if 0 <= i - 1 < NB:
@@ -242,11 +244,13 @@ def tile_fusionfeature_layer_kernel(tc, query_feature, support_feature, out_0, o
             for j in range(8):
                 if i < NB:
                     adj_evac(i, j)
+                if j == 3 and 0 <= i - 4 < NB:
+                    mx(i - 4)
                 if 0 <= i - 2 < NB:
                     for s in range(4 * j, 4 * j + 4):
                         transp(i - 2, s)
-                if j == 5 and 0 <= i - 4 < NB:
-                    mx(i - 4)
+                    if j == 3:
+                        copyout(i - 2, 0)
             if i == 0:
                 for kb in range(1, 4):
                     qft_bank(kb)
@@ -257,10 +261,8 @@ def tile_fusionfeature_layer_kernel(tc, query_feature, support_feature, out_0, o
             if i == 2:
                 gate_finish()
             if 0 <= i - 2 < NB:
-                for k in range(4):
+                for k in range(1, 4):
                     copyout(i - 2, k)
-            if 0 <= i - 4 < NB:
-                epi(i - 4)
             if i == NB:
                 for ch in range(1, 4):
                     out1_piece(ch)

@@ -22,7 +22,7 @@ G = N // 512
 FLOPS = 2 * 2 * N * N * C
 
 MANUAL = True
-POLICY = [("V", True), ("A", True), ("A", True), ("A", True)]
+POLICY = [("V", False), ("A", False), ("A", False), ("A", False)]
 
 
 def tile_fusionfeature_layer_kernel(tc, query_feature, support_feature, out_0, out_1):

@@ -22,7 +22,7 @@ G = N // 512
 FLOPS = 2 * 2 * N * N * C
 
 MANUAL = True
-POLICY = [("V", False), ("A", False), ("A", False), ("A", False)]
+POLICY = [("V", True), ("A", False), ("V", True), ("A", False)]
 
 
 def tile_fusionfeature_layer_kernel(tc, query_feature, support_feature, out_0, out_1):
@@ -251,6 +251,8 @@ def tile_fusionfeature_layer_kernel(tc, query_feature, support_feature, out_0, o
                         transp(i - 2, s)
                     if j == 3:
                         copyout(i - 2, 0)
+                    if j == 6:
+                        copyout(i - 2, 2)
             if i == 0:
                 for kb in range(1, 4):
                     qft_bank(kb)
@@ -261,7 +263,7 @@ def tile_fusionfeature_layer_kernel(tc, query_feature, support_feature, out_0, o
             if i == 2:
                 gate_finish()
             if 0 <= i - 2 < NB:
-                for k in range(1, 4):
+                for k in (1, 3):
                     copyout(i - 2, k)
             if i == NB:
                 for ch in range(1, 4):

@@ -1,8 +1,6 @@
 from contextlib import ExitStack
 
-import concourse.bass as bass
 import concourse.mybir as mybir
-import concourse.tile as tile
 from concourse.masks import make_identity
 
 F32 = mybir.dt.float32
@@ -18,11 +16,10 @@ P = 128
 N = 4096
 C = 128
 NB = N // P
-G = N // 512
+K_PASS = 512
+G = N // K_PASS
+BANK = 1024
 FLOPS = 2 * 2 * N * N * C
-
-MANUAL = True
-POLICY = [("V", True), ("A", False), ("V", True), ("A", False)]
 
 
 def tile_fusionfeature_layer_kernel(tc, query_feature, support_feature, out_0, out_1):
@@ -36,16 +33,16 @@ def tile_fusionfeature_layer_kernel(tc, query_feature, support_feature, out_0, o
     with ExitStack() as ctx:
         const = ctx.enter_context(tc.tile_pool(name="const", bufs=1))
         work = ctx.enter_context(tc.tile_pool(name="work", bufs=2))
-        psum = ctx.enter_context(tc.psum_pool(name="psum", bufs=2))
-        if MANUAL:
-            ctx.enter_context(tc.manual_schedule())
+        psum = ctx.enter_context(tc.psum_pool(name="psum", bufs=1))
+        ctx.enter_context(tc.manual_schedule())
 
         ident = const.tile([P, P], BF16, name="ident")
         make_identity(nc, ident[:])
 
         q_nat = const.tile([P, N], BF16, name="q_nat")
         s_nat = const.tile([P, N], BF16, name="s_nat")
-        qmx_raw = const.tile([P, G, 512], BF16, name="qmx_raw")
+        qmx_raw = const.tile([P, G, K_PASS], BF16, name="qmx_raw")
+
         def load(dst, src, ch):
             cols = slice(ch * 1024, (ch + 1) * 1024)
             nc.sync.dma_start(out=dst[:, cols], in_=src[:, cols])
@@ -60,39 +57,33 @@ def tile_fusionfeature_layer_kernel(tc, query_feature, support_feature, out_0, o
         qfT = const.tile([P, N], BF16, name="qfT")
 
         def qft_bank(kb):
-            tq = psum.tile([P, 1024], BF16, name="tq", tag="tp", bufs=3)
+            tq = psum.tile([P, BANK], BF16, name="tq", tag="tp", bufs=3)
             for r in range(8):
                 b = kb * 8 + r
                 nc.tensor.transpose(tq[:, r * P:(r + 1) * P], q_nat[:, b * P:(b + 1) * P], ident[:])
             if kb == 0:
-                nc.vector.tensor_copy(out=qfT[:, kb * 1024:(kb + 1) * 1024], in_=tq[:])
+                nc.vector.tensor_copy(out=qfT[:, kb * BANK:(kb + 1) * BANK], in_=tq[:])
             else:
-                nc.scalar.copy(out=qfT[:, kb * 1024:(kb + 1) * 1024], in_=tq[:])
+                nc.scalar.copy(out=qfT[:, kb * BANK:(kb + 1) * BANK], in_=tq[:])
 
         qft_bank(0)
 
         sfp = const.tile([P, N], BF16, name="sfp")
+        spart = const.tile([P, G], F32, name="spart")
         for g in range(G):
-            cols = slice(g * 512, (g + 1) * 512)
-            dst = sfp[:, cols].rearrange("c (t p) -> c t p", t=4)
-            src = s_nat[:, cols].rearrange("c (p t) -> c t p", t=4)
-            if g == 0:
-                nc.vector.tensor_copy(out=dst, in_=src)
-            else:
-                nc.scalar.copy(out=dst, in_=src)
-
-        tree = const.tile([P, 2048], F32, name="tree")
-        nc.gpsimd.tensor_tensor(out=tree[:], in0=s_nat[:, 0:2048], in1=s_nat[:, 2048:4096], op=ALU.add)
-        for wd in (1024, 512, 256, 128, 64):
-            nc.gpsimd.tensor_tensor(out=tree[:, 0:wd], in0=tree[:, 0:wd], in1=tree[:, wd:2 * wd], op=ALU.add)
+            cols = slice(g * K_PASS, (g + 1) * K_PASS)
+            nc.scalar.activation(out=sfp[:, cols].rearrange("c (t p) -> c t p", t=4),
+                                 in_=s_nat[:, cols].rearrange("c (p t) -> c t p", t=4),
+                                 func=ACTF.Copy, accum_out=spart[:, g:g + 1])
 
         qgrp = const.tile([P, N], BF16, name="qgrp", align_bytes=64)
-        nc.gpsimd.tensor_scalar(
-            out=qgrp[:].rearrange("p (g c t) -> p g c t", g=G, t=4),
-            in0=qmx_raw[:].rearrange("p g (t c) -> p g c t", t=4),
-            scalar1=1.0, scalar2=0.0, op0=ALU.mult, op1=ALU.add)
         qcodes = const.tile([P, G * C], U32, name="qcodes", align_bytes=64)
         qscl = const.tile([P, G * C], U8, name="qscl", align_bytes=64)
+
+        def quantise_qf():
+            nc.vector.tensor_copy(out=qgrp[:].rearrange("p (g c t) -> p g c t", g=G, t=4),
+                                  in_=qmx_raw[:].rearrange("p g (t c) -> p g c t", t=4))
+            nc.vector.quantize_mx(out=qcodes[:].bitcast(FP8X4), scales=qscl[:], in_=qgrp[:])
 
         ssum = const.tile([P, 1], F32, name="ssum")
         ssp = const.tile([P, 32], BF16, name="ssp")
@@ -107,7 +98,7 @@ def tile_fusionfeature_layer_kernel(tc, query_feature, support_feature, out_0, o
         nc.vector.memset(ssp[:], 0.0)
 
         def gate_split():
-            nc.vector.tensor_reduce(out=ssum[:], in_=tree[:, 0:64], axis=AX.X, op=ALU.add)
+            nc.vector.tensor_reduce(out=ssum[:], in_=spart[:], axis=AX.X, op=ALU.add)
             nc.vector.tensor_copy(out=ssp[:, 0:1], in_=ssum[:])
             nc.vector.tensor_tensor(out=res1[:], in0=ssum[:], in1=ssp[:, 0:1], op=ALU.subtract)
             nc.vector.tensor_copy(out=ssp[:, 1:2], in_=res1[:])
@@ -171,31 +162,18 @@ def tile_fusionfeature_layer_kernel(tc, query_feature, support_feature, out_0, o
         def transp(b, s):
             k, r = divmod(s, 8)
             if r == 0:
-                st["tp", b, k] = psum.tile([P, 1024], BF16, name="tp", tag="tp", bufs=3)
+                st["tp", b, k] = psum.tile([P, BANK], BF16, name="tp", tag="tp", bufs=3)
             nc.tensor.transpose(st["tp", b, k][:, r * P:(r + 1) * P], st["e", b][:, s * P:(s + 1) * P], ident[:])
 
-        def copyout(b, k):
+        def regroup(b, k):
             if k == 0:
                 st["grp", b] = work.tile([P, N], BF16, name="grp", tag="grp", bufs=2, align_bytes=64)
-                st["pl", b] = work.tile([P, N], BF16, name="pl", tag="pl", bufs=2)
-            eng, via = POLICY[k]
-            cols = slice(k * 1024, (k + 1) * 1024)
-            tp = st["tp", b, k]
-            gdst = st["grp", b][:, cols].rearrange("p (g n t) -> p g n t", g=2, t=4)
-            if via:
-                dst = st["pl", b][:, cols]
-                src = tp[:]
-            else:
-                dst = gdst
-                src = tp[:].rearrange("p (g t n) -> p g n t", g=2, t=4)
-            if eng == "A":
-                nc.scalar.copy(out=dst, in_=src)
-            else:
+            dst = st["grp", b][:, k * BANK:(k + 1) * BANK].rearrange("p (g n t) -> p g n t", g=2, t=4)
+            src = st["tp", b, k][:].rearrange("p (g t n) -> p g n t", g=2, t=4)
+            if k == 0:
                 nc.vector.tensor_copy(out=dst, in_=src)
-            if via:
-                nc.gpsimd.tensor_scalar(out=gdst,
-                                        in0=st["pl", b][:, cols].rearrange("p (g t n) -> p g n t", g=2, t=4),
-                                        scalar1=1.0, scalar2=0.0, op0=ALU.mult, op1=ALU.add)
+            else:
+                nc.scalar.copy(out=dst, in_=src)
 
         def quant(b):
             codes = work.tile([P, G * P], U32, name="codes", tag="codes", bufs=2, align_bytes=64)
@@ -228,7 +206,7 @@ def tile_fusionfeature_layer_kernel(tc, query_feature, support_feature, out_0, o
 
         for i in range(NB + 6):
             if i == 3:
-                nc.vector.quantize_mx(out=qcodes[:].bitcast(FP8X4), scales=qscl[:], in_=qgrp[:])
+                quantise_qf()
             if 0 <= i - 4 < NB:
                 quant(i - 4)
             if 0 <= i - 5 < NB:
@@ -250,9 +228,7 @@ def tile_fusionfeature_layer_kernel(tc, query_feature, support_feature, out_0, o
                     for s in range(4 * j, 4 * j + 4):
                         transp(i - 2, s)
                     if j == 3:
-                        copyout(i - 2, 0)
-                    if j == 6:
-                        copyout(i - 2, 2)
+                        regroup(i - 2, 0)
             if i == 0:
                 for kb in range(1, 4):
                     qft_bank(kb)
@@ -263,8 +239,8 @@ def tile_fusionfeature_layer_kernel(tc, query_feature, support_feature, out_0, o
             if i == 2:
                 gate_finish()
             if 0 <= i - 2 < NB:
-                for k in (1, 3):
-                    copyout(i - 2, k)
+                for k in range(1, 4):
+                    regroup(i - 2, k)
             if i == NB:
                 for ch in range(1, 4):
                     out1_piece(ch)

@@ -19,6 +19,7 @@ NB = N // P
 K_PASS = 512
 G = N // K_PASS
 BANK = 1024
+WBANK = 512
 FLOPS = 2 * 2 * N * N * C
 
 
@@ -38,6 +39,8 @@ def tile_fusionfeature_layer_kernel(tc, query_feature, support_feature, out_0, o
 
         ident = const.tile([P, P], BF16, name="ident")
         make_identity(nc, ident[:])
+        ident_w = const.tile([P, P], F32, name="ident_w")
+        make_identity(nc, ident_w[:])
 
         q_nat = const.tile([P, N], BF16, name="q_nat")
         s_nat = const.tile([P, N], BF16, name="s_nat")
@@ -72,8 +75,8 @@ def tile_fusionfeature_layer_kernel(tc, query_feature, support_feature, out_0, o
         spart = const.tile([P, G], F32, name="spart")
         for g in range(G):
             cols = slice(g * K_PASS, (g + 1) * K_PASS)
-            nc.scalar.activation(out=sfp[:, cols].rearrange("c (t p) -> c t p", t=4),
-                                 in_=s_nat[:, cols].rearrange("c (p t) -> c t p", t=4),
+            nc.scalar.activation(out=sfp[:, cols].rearrange("c (u p e) -> c u p e", u=2, e=2),
+                                 in_=s_nat[:, cols].rearrange("c (p u e) -> c u p e", u=2, e=2),
                                  func=ACTF.Copy, accum_out=spart[:, g:g + 1])
 
         qgrp = const.tile([P, N], BF16, name="qgrp", align_bytes=64)
@@ -160,20 +163,19 @@ def tile_fusionfeature_layer_kernel(tc, query_feature, support_feature, out_0, o
                                  scale=1.0, accum_out=rs[:, b:b + 1])
 
         def transp(b, s):
-            k, r = divmod(s, 8)
+            k, r = divmod(s, 4)
             if r == 0:
-                st["tp", b, k] = psum.tile([P, BANK], BF16, name="tp", tag="tp", bufs=3)
-            nc.tensor.transpose(st["tp", b, k][:, r * P:(r + 1) * P], st["e", b][:, s * P:(s + 1) * P], ident[:])
+                st["tp", b, k] = psum.tile([P, WBANK], F32, name="tp", tag="tp", bufs=3)
+            words = st["e", b][:].bitcast(F32)
+            nc.tensor.transpose(st["tp", b, k][:, r * P:(r + 1) * P], words[:, s * P:(s + 1) * P], ident_w[:])
 
         def regroup(b, k):
             if k == 0:
                 st["grp", b] = work.tile([P, N], BF16, name="grp", tag="grp", bufs=2, align_bytes=64)
-            dst = st["grp", b][:, k * BANK:(k + 1) * BANK].rearrange("p (g n t) -> p g n t", g=2, t=4)
-            src = st["tp", b, k][:].rearrange("p (g t n) -> p g n t", g=2, t=4)
-            if k == 0:
-                nc.vector.tensor_copy(out=dst, in_=src)
-            else:
-                nc.scalar.copy(out=dst, in_=src)
+            words = st["grp", b][:].bitcast(F32)
+            dst = words[:, k * WBANK:(k + 1) * WBANK].rearrange("p (g n u) -> p g n u", g=2, u=2)
+            src = st["tp", b, k][:].rearrange("p (g u n) -> p g n u", g=2, u=2)
+            nc.scalar.copy(out=dst, in_=src)
 
         def quant(b):
             codes = work.tile([P, G * P], U32, name="codes", tag="codes", bufs=2, align_bytes=64)
@@ -225,10 +227,8 @@ def tile_fusionfeature_layer_kernel(tc, query_feature, support_feature, out_0, o
                 if j == 3 and 0 <= i - 4 < NB:
                     mx(i - 4)
                 if 0 <= i - 2 < NB:
-                    for s in range(4 * j, 4 * j + 4):
+                    for s in range(2 * j, 2 * j + 2):
                         transp(i - 2, s)
-                    if j == 3:
-                        regroup(i - 2, 0)
             if i == 0:
                 for kb in range(1, 4):
                     qft_bank(kb)
@@ -239,7 +239,7 @@ def tile_fusionfeature_layer_kernel(tc, query_feature, support_feature, out_0, o
             if i == 2:
                 gate_finish()
             if 0 <= i - 2 < NB:
-                for k in range(1, 4):
+                for k in range(4):
                     regroup(i - 2, k)
             if i == NB:
                 for ch in range(1, 4):

@@ -83,9 +83,11 @@ def tile_fusionfeature_layer_kernel(tc, query_feature, support_feature, out_0, o
         qcodes = const.tile([P, G * C], U32, name="qcodes", align_bytes=64)
         qscl = const.tile([P, G * C], U8, name="qscl", align_bytes=64)
 
-        def quantise_qf():
+        def regroup_qf():
             nc.vector.tensor_copy(out=qgrp[:].rearrange("p (g c t) -> p g c t", g=G, t=4),
                                   in_=qmx_raw[:].rearrange("p g (t c) -> p g c t", t=4))
+
+        def quantise_qf():
             nc.vector.quantize_mx(out=qcodes[:].bitcast(FP8X4), scales=qscl[:], in_=qgrp[:])
 
         ssum = const.tile([P, 1], F32, name="ssum")
@@ -100,13 +102,14 @@ def tile_fusionfeature_layer_kernel(tc, query_feature, support_feature, out_0, o
         o1 = const.tile([P, N], F32, name="o1")
         nc.vector.memset(ssp[:], 0.0)
 
-        def gate_split():
-            nc.vector.tensor_reduce(out=ssum[:], in_=spart[:], axis=AX.X, op=ALU.add)
-            nc.vector.tensor_copy(out=ssp[:, 0:1], in_=ssum[:])
-            nc.vector.tensor_tensor(out=res1[:], in0=ssum[:], in1=ssp[:, 0:1], op=ALU.subtract)
-            nc.vector.tensor_copy(out=ssp[:, 1:2], in_=res1[:])
-            nc.vector.tensor_tensor(out=res2[:], in0=res1[:], in1=ssp[:, 1:2], op=ALU.subtract)
-            nc.vector.tensor_copy(out=ssp[:, 2:3], in_=res2[:])
+        gate_split = [
+            lambda: nc.vector.tensor_reduce(out=ssum[:], in_=spart[:], axis=AX.X, op=ALU.add),
+            lambda: nc.vector.tensor_copy(out=ssp[:, 0:1], in_=ssum[:]),
+            lambda: nc.vector.tensor_tensor(out=res1[:], in0=ssum[:], in1=ssp[:, 0:1], op=ALU.subtract),
+            lambda: nc.vector.tensor_copy(out=ssp[:, 1:2], in_=res1[:]),
+            lambda: nc.vector.tensor_tensor(out=res2[:], in0=res1[:], in1=ssp[:, 1:2], op=ALU.subtract),
+            lambda: nc.vector.tensor_copy(out=ssp[:, 2:3], in_=res2[:]),
+        ]
 
         def gate_matmuls():
             for hb in range(2):
@@ -122,10 +125,11 @@ def tile_fusionfeature_layer_kernel(tc, query_feature, support_feature, out_0, o
         def gate_exp():
             nc.scalar.activation(out=gexp[:], in_=vsum[:], func=ACTF.Exp, scale=-1.0)
 
-        def gate_finish():
-            nc.vector.tensor_scalar_add(out=gden[:], in0=gexp[:], scalar1=1.0)
-            nc.vector.reciprocal(out=gate[:], in_=gden[:])
-            nc.vector.tensor_scalar_add(out=gate1[:], in0=gate[:], scalar1=1.0)
+        gate_finish = [
+            lambda: nc.vector.tensor_scalar_add(out=gden[:], in0=gexp[:], scalar1=1.0),
+            lambda: nc.vector.reciprocal(out=gate[:], in_=gden[:]),
+            lambda: nc.vector.tensor_scalar_add(out=gate1[:], in0=gate[:], scalar1=1.0),
+        ]
 
         def out1_piece(ch):
             cols = slice(ch * 1024, (ch + 1) * 1024)
@@ -194,53 +198,62 @@ def tile_fusionfeature_layer_kernel(tc, query_feature, support_feature, out_0, o
                                     rhs=qcodes[:, cols].bitcast(FP8X4), rhs_scale=qscl[:, cols],
                                     start=(g == 0), stop=(g == G - 1))
 
-        def epi(b):
-            rinv = work.tile([P, 1], F32, name="rinv", tag="rinv", bufs=3)
-            wgt = work.tile([P, 1], F32, name="wgt", tag="wgt", bufs=3)
-            nc.vector.reciprocal(out=rinv[:], in_=rs[:, b:b + 1])
-            nc.vector.tensor_tensor(out=wgt[:], in0=rinv[:], in1=gate[:, b:b + 1], op=ALU.mult)
+        def epi_recip(b):
+            st["rinv", b] = work.tile([P, 1], F32, name="rinv", tag="rinv", bufs=3)
+            nc.vector.reciprocal(out=st["rinv", b][:], in_=rs[:, b:b + 1])
+
+        def epi_weight(b):
+            st["wgt", b] = work.tile([P, 1], F32, name="wgt", tag="wgt", bufs=3)
+            nc.vector.tensor_tensor(out=st["wgt", b][:], in0=st["rinv", b][:], in1=gate[:, b:b + 1], op=ALU.mult)
+
+        def epi_out(b):
             cols = slice(b * P, (b + 1) * P)
-            nc.vector.scalar_tensor_tensor(out=o0[:, cols], in0=st["acc", b][:], scalar=wgt[:], in1=q_nat[:, cols],
-                                           op0=ALU.mult, op1=ALU.add)
+            nc.vector.scalar_tensor_tensor(out=o0[:, cols], in0=st["acc", b][:], scalar=st["wgt", b][:],
+                                           in1=q_nat[:, cols], op0=ALU.mult, op1=ALU.add)
             if b % 4 == 3:
                 cc = slice((b - 3) * P, (b + 1) * P)
                 nc.sync.dma_start(out=o0_d[:, cc], in_=o0[:, cc])
 
-        for i in range(NB + 6):
-            if i == 3:
+        def between(i, j):
+            if j == 0 and 0 <= i - 1 < NB:
+                negmax(i - 1)
+            if i == 1 and j < len(gate_split):
+                gate_split[j]()
+            if i == 2 and j == 3:
+                regroup_qf()
+            if i == 3 and j == 1:
                 quantise_qf()
+            if i == 3 and j >= 5:
+                gate_finish[j - 5]()
             if 0 <= i - 4 < NB:
-                quant(i - 4)
-            if 0 <= i - 5 < NB:
-                epi(i - 5)
+                if j == 1:
+                    epi_recip(i - 4)
+                if j == 2:
+                    epi_weight(i - 4)
+                if j == 4:
+                    epi_out(i - 4)
+            if j == 3 and 0 <= i - 3 < NB:
+                quant(i - 3)
+
+        for i in range(NB + 4):
+            if 0 <= i - 4 < NB:
+                mx(i - 4)
             if i == 2:
                 gate_matmuls()
-            if 0 <= i - 1 < NB:
-                expo(i - 1)
-            if i == 2:
-                gate_exp()
-            if i == NB:
-                out1_piece(0)
             for j in range(8):
                 if i < NB:
                     adj_evac(i, j)
-                if j == 3 and 0 <= i - 4 < NB:
-                    mx(i - 4)
-                if 0 <= i - 2 < NB:
-                    for s in range(2 * j, 2 * j + 2):
+                between(i, j)
+                if j == 0 and 0 <= i - 1 < NB:
+                    expo(i - 1)
+                    if i == 2:
+                        gate_exp()
+                if 0 <= i - 2 < NB and j % 2 == 1:
+                    for s in range(2 * j - 2, 2 * j + 2):
                         transp(i - 2, s)
+                    regroup(i - 2, j // 2)
+                if i == NB and j % 2 == 1:
+                    out1_piece(j // 2)
             if i == 0:
                 for kb in range(1, 4):
                     qft_bank(kb)
-            if i < NB:
-                negmax(i)
-            if i == 1:
-                gate_split()
-            if i == 2:
-                gate_finish()
-            if 0 <= i - 2 < NB:
-                for k in range(4):
-                    regroup(i - 2, k)
-            if i == NB:
-                for ch in range(1, 4):
-                    out1_piece(ch)

@@ -46,30 +46,25 @@ def tile_fusionfeature_layer_kernel(tc, query_feature, support_feature, out_0, o
         s_nat = const.tile([P, N], BF16, name="s_nat")
         qmx_raw = const.tile([P, G, K_PASS], BF16, name="qmx_raw")
 
-        def load(dst, src, ch):
-            cols = slice(ch * 1024, (ch + 1) * 1024)
-            nc.sync.dma_start(out=dst[:, cols], in_=src[:, cols])
+        def load(dst, src, lo, hi):
+            nc.sync.dma_start(out=dst[:, lo:hi], in_=src[:, lo:hi])
 
-        load(q_nat, q_d, 0)
-        for ch in range(4):
-            load(s_nat, s_d, ch)
+        load(q_nat, q_d, 0, 512)
+        for lo, hi in ((0, 512), (512, 1024), (1024, 2048), (2048, 3072), (3072, 4096)):
+            load(s_nat, s_d, lo, hi)
+        for lo, hi in ((512, 2048), (2048, 4096)):
+            load(q_nat, q_d, lo, hi)
         nc.sync.dma_start(out=qmx_raw[:], in_=qmx_d)
-        for ch in range(1, 4):
-            load(q_nat, q_d, ch)
 
         qfT = const.tile([P, N], BF16, name="qfT")
 
-        def qft_bank(kb):
-            tq = psum.tile([P, BANK], BF16, name="tq", tag="tp", bufs=3)
-            for r in range(8):
-                b = kb * 8 + r
-                nc.tensor.transpose(tq[:, r * P:(r + 1) * P], q_nat[:, b * P:(b + 1) * P], ident[:])
-            if kb == 0:
-                nc.vector.tensor_copy(out=qfT[:, kb * BANK:(kb + 1) * BANK], in_=tq[:])
-            else:
-                nc.scalar.copy(out=qfT[:, kb * BANK:(kb + 1) * BANK], in_=tq[:])
+        def qft_blocks(lo, hi, engine_copy):
+            tq = psum.tile([P, BANK], BF16, name="tq", tag="tp", bufs=4)
+            for b in range(lo, hi):
+                nc.tensor.transpose(tq[:, (b - lo) * P:(b - lo + 1) * P], q_nat[:, b * P:(b + 1) * P], ident[:])
+            engine_copy(out=qfT[:, lo * P:hi * P], in_=tq[:, 0:(hi - lo) * P])
 
-        qft_bank(0)
+        qft_blocks(0, 4, nc.vector.tensor_copy)
 
         sfp = const.tile([P, N], BF16, name="sfp")
         spart = const.tile([P, G], F32, name="spart")
@@ -113,7 +108,7 @@ def tile_fusionfeature_layer_kernel(tc, query_feature, support_feature, out_0, o
 
         def gate_matmuls():
             for hb in range(2):
-                gp = psum.tile([P, 512], F32, name="gp", tag="adj", bufs=4)
+                gp = psum.tile([P, 512], F32, name="gp", tag="adj", bufs=3)
                 for r in range(16):
                     b = hb * 16 + r
                     nc.tensor.matmul(out=gp[:, r * 32:(r + 1) * 32], lhsT=qfT[:, b * P:(b + 1) * P], rhs=ssp[:],
@@ -131,14 +126,13 @@ def tile_fusionfeature_layer_kernel(tc, query_feature, support_feature, out_0, o
             lambda: nc.vector.tensor_scalar_add(out=gate1[:], in0=gate[:], scalar1=1.0),
         ]
 
-        def out1_piece(ch):
-            cols = slice(ch * 1024, (ch + 1) * 1024)
-            nc.vector.tensor_tensor(
-                out=o1[:, cols].rearrange("p (b k) -> p b k", k=P),
-                in0=s_nat[:, cols].rearrange("p (b k) -> p b k", k=P),
-                in1=gate1[:, ch * 8:(ch + 1) * 8].unsqueeze(2).to_broadcast([P, 8, P]),
-                op=ALU.mult)
-            nc.sync.dma_start(out=o1_d[:, cols], in_=o1[:, cols])
+        def out1_block(b):
+            cols = slice(b * P, (b + 1) * P)
+            nc.gpsimd.tensor_scalar(out=o1[:, cols], in0=s_nat[:, cols], scalar1=gate1[:, b:b + 1], scalar2=0.0,
+                                    op0=ALU.mult, op1=ALU.add)
+            if b % 8 == 7:
+                cc = slice((b - 7) * P, (b + 1) * P)
+                nc.sync.dma_start(out=o1_d[:, cc], in_=o1[:, cc])
 
         o0 = const.tile([P, N], F32, name="o0")
         rs = const.tile([P, NB], F32, name="rs")
@@ -148,7 +142,7 @@ def tile_fusionfeature_layer_kernel(tc, query_feature, support_feature, out_0, o
             if j == 0:
                 st["adjs", b] = work.tile([P, N], F32, name="adjs", tag="adjs", bufs=3)
                 st["mx8", b] = work.tile([P, 8], F32, name="mx8", tag="mx8", bufs=3)
-            ap = psum.tile([P, 512], F32, name="ap", tag="adj", bufs=4)
+            ap = psum.tile([P, 512], F32, name="ap", tag="adj", bufs=3)
             nc.tensor.matmul(out=ap[:], lhsT=qfT[:, b * P:(b + 1) * P], rhs=sfp[:, j * 512:(j + 1) * 512],
                              start=True, stop=True)
             nc.vector.tensor_scalar(out=st["adjs", b][:, j * 512:(j + 1) * 512], in0=ap[:], scalar1=1.0,
@@ -166,56 +160,69 @@ def tile_fusionfeature_layer_kernel(tc, query_feature, support_feature, out_0, o
             nc.scalar.activation(out=e[:], in_=st["adjs", b][:], func=ACTF.Exp, bias=st["nm", b][:],
                                  scale=1.0, accum_out=rs[:, b:b + 1])
 
+        rs_last = const.tile([P, 4], F32, name="rs_last")
+
+        def expo_last(k):
+            b = NB - 1
+            if k == 0:
+                st["e", b] = work.tile([P, N], BF16, name="e", tag="e", bufs=2)
+            cols = slice(k * BANK, (k + 1) * BANK)
+            nc.scalar.activation(out=st["e", b][:, cols], in_=st["adjs", b][:, cols], func=ACTF.Exp,
+                                 bias=st["nm", b][:], scale=1.0, accum_out=rs_last[:, k:k + 1])
+
         def transp(b, s):
             k, r = divmod(s, 4)
             if r == 0:
-                st["tp", b, k] = psum.tile([P, WBANK], F32, name="tp", tag="tp", bufs=3)
+                st["tp", b, k] = psum.tile([P, WBANK], F32, name="tp", tag="tp", bufs=4)
             words = st["e", b][:].bitcast(F32)
             nc.tensor.transpose(st["tp", b, k][:, r * P:(r + 1) * P], words[:, s * P:(s + 1) * P], ident_w[:])
 
-        def regroup(b, k):
+        def regroup(b, k, engine_copy=nc.scalar.copy):
             if k == 0:
                 st["grp", b] = work.tile([P, N], BF16, name="grp", tag="grp", bufs=2, align_bytes=64)
             words = st["grp", b][:].bitcast(F32)
             dst = words[:, k * WBANK:(k + 1) * WBANK].rearrange("p (g n u) -> p g n u", g=2, u=2)
             src = st["tp", b, k][:].rearrange("p (g u n) -> p g n u", g=2, u=2)
-            nc.scalar.copy(out=dst, in_=src)
+            engine_copy(out=dst, in_=src)
 
-        def quant(b):
-            codes = work.tile([P, G * P], U32, name="codes", tag="codes", bufs=2, align_bytes=64)
-            scl = work.tile([P, G * P], U8, name="scl", tag="scl", bufs=2, align_bytes=64)
-            st["codes", b] = codes
-            st["scl", b] = scl
-            nc.vector.quantize_mx(out=codes[:].bitcast(FP8X4), scales=scl[:], in_=st["grp", b][:])
+        def quant(b, lo=0, hi=G):
+            if lo == 0:
+                st["codes", b] = work.tile([P, G * P], U32, name="codes", tag="codes", bufs=2, align_bytes=64)
+                st["scl", b] = work.tile([P, G * P], U8, name="scl", tag="scl", bufs=2, align_bytes=64)
+            cols = slice(lo * P, hi * P)
+            nc.vector.quantize_mx(out=st["codes", b][:, cols].bitcast(FP8X4), scales=st["scl", b][:, cols],
+                                  in_=st["grp", b][:, lo * K_PASS:hi * K_PASS])
 
-        def mx(b):
-            acc = psum.tile([P, C], F32, name="acc", tag="acc", bufs=1)
-            st["acc", b] = acc
-            for g in range(G):
+        def mx(b, lo=0, hi=G):
+            if lo == 0:
+                st["acc", b] = psum.tile([P, C], F32, name="acc", tag="acc", bufs=1)
+            for g in range(lo, hi):
                 cols = slice(g * P, (g + 1) * P)
-                nc.tensor.matmul_mx(out=acc[:], lhsT=st["codes", b][:, cols].bitcast(FP8X4),
+                nc.tensor.matmul_mx(out=st["acc", b][:], lhsT=st["codes", b][:, cols].bitcast(FP8X4),
                                     lhsT_scale=st["scl", b][:, cols],
                                     rhs=qcodes[:, cols].bitcast(FP8X4), rhs_scale=qscl[:, cols],
                                     start=(g == 0), stop=(g == G - 1))
 
-        def epi_recip(b):
-            st["rinv", b] = work.tile([P, 1], F32, name="rinv", tag="rinv", bufs=3)
-            nc.vector.reciprocal(out=st["rinv", b][:], in_=rs[:, b:b + 1])
+        rinv = const.tile([P, NB], F32, name="rinv")
+        wgt = const.tile([P, NB], F32, name="wgt")
 
-        def epi_weight(b):
-            st["wgt", b] = work.tile([P, 1], F32, name="wgt", tag="wgt", bufs=3)
-            nc.vector.tensor_tensor(out=st["wgt", b][:], in0=st["rinv", b][:], in1=gate[:, b:b + 1], op=ALU.mult)
+        def epi_recip(lo, hi):
+            nc.vector.reciprocal(out=rinv[:, lo:hi], in_=rs[:, lo:hi])
+
+        def epi_weight(lo, hi, engine):
+            engine.tensor_tensor(out=wgt[:, lo:hi], in0=rinv[:, lo:hi], in1=gate[:, lo:hi], op=ALU.mult)
 
         def epi_out(b):
             cols = slice(b * P, (b + 1) * P)
-            nc.vector.scalar_tensor_tensor(out=o0[:, cols], in0=st["acc", b][:], scalar=st["wgt", b][:],
+            nc.vector.scalar_tensor_tensor(out=o0[:, cols], in0=st["acc", b][:], scalar=wgt[:, b:b + 1],
                                            in1=q_nat[:, cols], op0=ALU.mult, op1=ALU.add)
-            if b % 4 == 3:
-                cc = slice((b - 3) * P, (b + 1) * P)
+            if b % 4 == 3 or b == NB - 2:
+                first = b - 2 if b == NB - 2 else (b if b == NB - 1 else b - 3)
+                cc = slice(first * P, (b + 1) * P)
                 nc.sync.dma_start(out=o0_d[:, cc], in_=o0[:, cc])
 
         def between(i, j):
-            if j == 0 and 0 <= i - 1 < NB:
+            if j == 0 and i >= 2:
                 negmax(i - 1)
             if i == 1 and j < len(gate_split):
                 gate_split[j]()
@@ -226,34 +233,74 @@ def tile_fusionfeature_layer_kernel(tc, query_feature, support_feature, out_0, o
             if i == 3 and j >= 5:
                 gate_finish[j - 5]()
             if 0 <= i - 4 < NB:
-                if j == 1:
-                    epi_recip(i - 4)
-                if j == 2:
-                    epi_weight(i - 4)
+                if j == 1 and i % 2 == 0:
+                    epi_recip(i - 4, i - 2)
+                    epi_weight(i - 4, i - 2, nc.gpsimd)
                 if j == 4:
                     epi_out(i - 4)
             if j == 3 and 0 <= i - 3 < NB:
                 quant(i - 3)
 
-        for i in range(NB + 4):
-            if 0 <= i - 4 < NB:
+        for i in range(NB):
+            if 0 <= i - 4:
                 mx(i - 4)
+                out1_block(i - 4)
             if i == 2:
                 gate_matmuls()
             for j in range(8):
-                if i < NB:
-                    adj_evac(i, j)
+                adj_evac(i, j)
                 between(i, j)
-                if j == 0 and 0 <= i - 1 < NB:
+                if j == 0 and 0 <= i - 1:
                     expo(i - 1)
                     if i == 2:
                         gate_exp()
-                if 0 <= i - 2 < NB and j % 2 == 1:
+                if 0 <= i - 2 and j % 2 == 1:
                     for s in range(2 * j - 2, 2 * j + 2):
                         transp(i - 2, s)
-                    regroup(i - 2, j // 2)
-                if i == NB and j % 2 == 1:
-                    out1_piece(j // 2)
+                    if i < NB - 1 or j < 4:
+                        regroup(i - 2, j // 2)
             if i == 0:
-                for kb in range(1, 4):
-                    qft_bank(kb)
+                for lo in range(4, NB, 8):
+                    qft_blocks(lo, min(lo + 8, NB), nc.scalar.copy)
+                negmax(0)
+
+        for b in range(NB - 4, NB):
+            out1_block(b)
+        last = NB - 1
+        negmax(last)
+        mx(NB - 4)
+        epi_recip(NB - 4, NB - 2)
+        epi_weight(NB - 4, NB - 2, nc.gpsimd)
+        for k in range(4):
+            expo_last(k)
+        regroup(NB - 3, 2, nc.vector.tensor_copy)
+        regroup(NB - 3, 3, nc.vector.tensor_copy)
+        for s in range(16):
+            transp(NB - 2, s)
+        epi_out(NB - 4)
+        quant(NB - 3)
+        regroup(NB - 2, 0, nc.vector.tensor_copy)
+        regroup(NB - 2, 1, nc.vector.tensor_copy)
+        mx(NB - 3)
+        regroup(NB - 2, 2, nc.vector.tensor_copy)
+        regroup(NB - 2, 3, nc.vector.tensor_copy)
+        epi_out(NB - 3)
+        epi_recip(NB - 2, last)
+        quant(NB - 2)
+        epi_weight(NB - 2, last, nc.vector)
+        for s in range(16):
+            transp(last, s)
+        mx(NB - 2)
+        regroup(last, 0, nc.vector.tensor_copy)
+        regroup(last, 1, nc.vector.tensor_copy)
+        regroup(last, 2)
+        regroup(last, 3)
+        nc.vector.tensor_reduce(out=rs[:, last:NB], in_=rs_last[:], axis=AX.X, op=ALU.add)
+        quant(last, 0, G // 2)
+        epi_out(NB - 2)
+        mx(last, 0, G // 2)
+        epi_recip(last, NB)
+        quant(last, G // 2, G)
+        mx(last, G // 2, G)
+        epi_weight(last, NB, nc.vector)
+        epi_out(last)

@@ -78,9 +78,10 @@ def tile_fusionfeature_layer_kernel(tc, query_feature, support_feature, out_0, o
         qcodes = const.tile([P, G * C], U32, name="qcodes", align_bytes=64)
         qscl = const.tile([P, G * C], U8, name="qscl", align_bytes=64)
 
-        def regroup_qf():
-            nc.vector.tensor_copy(out=qgrp[:].rearrange("p (g c t) -> p g c t", g=G, t=4),
-                                  in_=qmx_raw[:].rearrange("p g (t c) -> p g c t", t=4))
+        def regroup_qf(g):
+            nc.gpsimd.tensor_scalar(out=qgrp[:, g * K_PASS:(g + 1) * K_PASS].rearrange("p (c t) -> p c t", t=4),
+                                    in0=qmx_raw[:, g, :].rearrange("p (t c) -> p c t", t=4),
+                                    scalar1=1.0, scalar2=0.0, op0=ALU.mult, op1=ALU.add)
 
         def quantise_qf():
             nc.vector.quantize_mx(out=qcodes[:].bitcast(FP8X4), scales=qscl[:], in_=qgrp[:])
@@ -148,6 +149,20 @@ def tile_fusionfeature_layer_kernel(tc, query_feature, support_feature, out_0, o
             nc.vector.tensor_scalar(out=st["adjs", b][:, j * 512:(j + 1) * 512], in0=ap[:], scalar1=1.0,
                                     scalar2=None, op0=ALU.mult, op1=ALU.max,
                                     accum_out=st["mx8", b][:, j:j + 1])
+
+        def fold_max(b, j):
+            mx8 = st["mx8", b]
+            if j == 1:
+                st["fold", b] = work.tile([P, 8], F32, name="fold", tag="fold", bufs=3)
+                st["nm", b] = work.tile([P, 1], F32, name="nm", tag="nm", bufs=3)
+            fold = st["fold", b]
+            before = mx8[:, 0:1] if j == 1 else fold[:, j - 1:j]
+            if j < 7:
+                nc.gpsimd.tensor_scalar(out=fold[:, j:j + 1], in0=mx8[:, j:j + 1], scalar1=before, scalar2=None,
+                                        op0=ALU.max)
+            else:
+                nc.gpsimd.tensor_scalar(out=st["nm", b][:], in0=mx8[:, j:j + 1], scalar1=before, scalar2=-1.0,
+                                        op0=ALU.max, op1=ALU.mult)
 
         def negmax(b):
             nm = work.tile([P, 1], F32, name="nm", tag="nm", bufs=3)
@@ -222,12 +237,12 @@ def tile_fusionfeature_layer_kernel(tc, query_feature, support_feature, out_0, o
                 nc.sync.dma_start(out=o0_d[:, cc], in_=o0[:, cc])
 
         def between(i, j):
-            if j == 0 and i >= 2:
-                negmax(i - 1)
+            if j == 0 and i == 2:
+                negmax(1)
+            if j >= 1 and i >= 2:
+                fold_max(i, j)
             if i == 1 and j < len(gate_split):
                 gate_split[j]()
-            if i == 2 and j == 3:
-                regroup_qf()
             if i == 3 and j == 1:
                 quantise_qf()
             if i == 3 and j >= 5:
@@ -250,6 +265,9 @@ def tile_fusionfeature_layer_kernel(tc, query_feature, support_feature, out_0, o
             for j in range(8):
                 adj_evac(i, j)
                 between(i, j)
+                if i == 0 and j >= 4:
+                    lo = 4 + (j - 4) * 8
+                    qft_blocks(lo, min(lo + 8, NB), nc.scalar.copy)
                 if j == 0 and 0 <= i - 1:
                     expo(i - 1)
                     if i == 2:
@@ -257,24 +275,20 @@ def tile_fusionfeature_layer_kernel(tc, query_feature, support_feature, out_0, o
                 if 0 <= i - 2 and j % 2 == 1:
                     for s in range(2 * j - 2, 2 * j + 2):
                         transp(i - 2, s)
-                    if i < NB - 1 or j < 4:
-                        regroup(i - 2, j // 2)
+                    regroup(i - 2, j // 2, nc.vector.tensor_copy if j == 1 and i % 6 == 0 else nc.scalar.copy)
             if i == 0:
-                for lo in range(4, NB, 8):
-                    qft_blocks(lo, min(lo + 8, NB), nc.scalar.copy)
                 negmax(0)
+                for g in range(G):
+                    regroup_qf(g)
 
-        for b in range(NB - 4, NB):
-            out1_block(b)
         last = NB - 1
-        negmax(last)
         mx(NB - 4)
         epi_recip(NB - 4, NB - 2)
         epi_weight(NB - 4, NB - 2, nc.gpsimd)
+        for b in range(NB - 4, NB):
+            out1_block(b)
         for k in range(4):
             expo_last(k)
-        regroup(NB - 3, 2, nc.vector.tensor_copy)
-        regroup(NB - 3, 3, nc.vector.tensor_copy)
         for s in range(16):
             transp(NB - 2, s)
         epi_out(NB - 4)
@@ -292,15 +306,16 @@ def tile_fusionfeature_layer_kernel(tc, query_feature, support_feature, out_0, o
             transp(last, s)
         mx(NB - 2)
         regroup(last, 0, nc.vector.tensor_copy)
-        regroup(last, 1, nc.vector.tensor_copy)
-        regroup(last, 2)
-        regroup(last, 3)
+        for k in range(1, 4):
+            regroup(last, k)
         nc.vector.tensor_reduce(out=rs[:, last:NB], in_=rs_last[:], axis=AX.X, op=ALU.add)
-        quant(last, 0, G // 2)
         epi_out(NB - 2)
-        mx(last, 0, G // 2)
         epi_recip(last, NB)
-        quant(last, G // 2, G)
-        mx(last, G // 2, G)
+        quant(last, 0, 4)
+        mx(last, 0, 4)
         epi_weight(last, NB, nc.vector)
+        quant(last, 4, 6)
+        mx(last, 4, 6)
+        quant(last, 6, 8)
+        mx(last, 6, 8)
         epi_out(last)

@@ -64,7 +64,8 @@ def tile_fusionfeature_layer_kernel(tc, query_feature, support_feature, out_0, o
                 nc.tensor.transpose(tq[:, (b - lo) * P:(b - lo + 1) * P], q_nat[:, b * P:(b + 1) * P], ident[:])
             engine_copy(out=qfT[:, lo * P:hi * P], in_=tq[:, 0:(hi - lo) * P])
 
-        qft_blocks(0, 4, nc.vector.tensor_copy)
+        qft_blocks(0, 1, nc.vector.tensor_copy)
+        qft_blocks(1, 4, nc.vector.tensor_copy)
 
         sfp = const.tile([P, N], BF16, name="sfp")
         spart = const.tile([P, G], F32, name="spart")
@@ -210,7 +211,8 @@ def tile_fusionfeature_layer_kernel(tc, query_feature, support_feature, out_0, o
 
         def mx(b, lo=0, hi=G):
             if lo == 0:
-                st["acc", b] = psum.tile([P, C], F32, name="acc", tag="acc", bufs=1)
+                tag, bufs = ("acc", 1) if b < NB - 2 else ("adj", 3)
+                st["acc", b] = psum.tile([P, C], F32, name="acc", tag=tag, bufs=bufs)
             for g in range(lo, hi):
                 cols = slice(g * P, (g + 1) * P)
                 nc.tensor.matmul_mx(out=st["acc", b][:], lhsT=st["codes", b][:, cols].bitcast(FP8X4),
@@ -275,7 +277,7 @@ def tile_fusionfeature_layer_kernel(tc, query_feature, support_feature, out_0, o
                 if 0 <= i - 2 and j % 2 == 1:
                     for s in range(2 * j - 2, 2 * j + 2):
                         transp(i - 2, s)
-                    regroup(i - 2, j // 2, nc.vector.tensor_copy if j == 1 and i % 6 == 0 else nc.scalar.copy)
+                    regroup(i - 2, j // 2, nc.vector.tensor_copy if j == 1 and i % 4 == 0 else nc.scalar.copy)
             if i == 0:
                 negmax(0)
                 for g in range(G):
@@ -291,10 +293,10 @@ def tile_fusionfeature_layer_kernel(tc, query_feature, support_feature, out_0, o
             expo_last(k)
         for s in range(16):
             transp(NB - 2, s)
-        epi_out(NB - 4)
-        quant(NB - 3)
         regroup(NB - 2, 0, nc.vector.tensor_copy)
+        epi_out(NB - 4)
         regroup(NB - 2, 1, nc.vector.tensor_copy)
+        quant(NB - 3)
         mx(NB - 3)
         regroup(NB - 2, 2, nc.vector.tensor_copy)
         regroup(NB - 2, 3, nc.vector.tensor_copy)
@@ -309,11 +311,11 @@ def tile_fusionfeature_layer_kernel(tc, query_feature, support_feature, out_0, o
         for k in range(1, 4):
             regroup(last, k)
         nc.vector.tensor_reduce(out=rs[:, last:NB], in_=rs_last[:], axis=AX.X, op=ALU.add)
-        epi_out(NB - 2)
         epi_recip(last, NB)
         quant(last, 0, 4)
         mx(last, 0, 4)
         epi_weight(last, NB, nc.vector)
+        epi_out(NB - 2)
         quant(last, 4, 6)
         mx(last, 4, 6)
         quant(last, 6, 8)

@@ -253,19 +253,20 @@ def tile_fusionfeature_layer_kernel(tc, query_feature, support_feature, out_0, o
                 if j == 1 and i % 2 == 0:
                     epi_recip(i - 4, i - 2)
                     epi_weight(i - 4, i - 2, nc.gpsimd)
-                if j == 4:
+                if j == 6:
                     epi_out(i - 4)
             if j == 3 and 0 <= i - 3 < NB:
                 quant(i - 3)
 
         for i in range(NB):
             if 0 <= i - 4:
-                mx(i - 4)
                 out1_block(i - 4)
             if i == 2:
                 gate_matmuls()
             for j in range(8):
                 adj_evac(i, j)
+                if j == 4 and 0 <= i - 4:
+                    mx(i - 4)
                 between(i, j)
                 if i == 0 and j >= 4:
                     lo = 4 + (j - 4) * 8

@@ -278,7 +278,9 @@ def tile_fusionfeature_layer_kernel(tc, query_feature, support_feature, out_0, o
                 if 0 <= i - 2 and j % 2 == 1:
                     for s in range(2 * j - 2, 2 * j + 2):
                         transp(i - 2, s)
-                    regroup(i - 2, j // 2, nc.vector.tensor_copy if j == 1 and i % 4 == 0 else nc.scalar.copy)
+                    if i == NB - 1 and j == 7:
+                        continue
+                    regroup(i - 2, j // 2, nc.vector.tensor_copy if j == 1 and i % 5 == 0 else nc.scalar.copy)
             if i == 0:
                 negmax(0)
                 for g in range(G):
@@ -292,6 +294,7 @@ def tile_fusionfeature_layer_kernel(tc, query_feature, support_feature, out_0, o
             out1_block(b)
         for k in range(4):
             expo_last(k)
+        regroup(NB - 3, 3, nc.vector.tensor_copy)
         for s in range(16):
             transp(NB - 2, s)
         regroup(NB - 2, 0, nc.vector.tensor_copy)
@@ -308,7 +311,7 @@ def tile_fusionfeature_layer_kernel(tc, query_feature, support_feature, out_0, o
         for s in range(16):
             transp(last, s)
         mx(NB - 2)
-        regroup(last, 0, nc.vector.tensor_copy)
+        regroup(last, 0)
         for k in range(1, 4):
             regroup(last, k)
         nc.vector.tensor_reduce(out=rs[:, last:NB], in_=rs_last[:], axis=AX.X, op=ALU.add)

@@ -20,6 +20,7 @@ K_PASS = 512
 G = N // K_PASS
 BANK = 1024
 WBANK = 512
+GN = 4
 FLOPS = 2 * 2 * N * N * C
 
 
@@ -49,8 +50,10 @@ def tile_fusionfeature_layer_kernel(tc, query_feature, support_feature, out_0, o
         def load(dst, src, lo, hi):
             nc.sync.dma_start(out=dst[:, lo:hi], in_=src[:, lo:hi])
 
-        load(q_nat, q_d, 0, 512)
-        for lo, hi in ((0, 512), (512, 1024), (1024, 2048), (2048, 3072), (3072, 4096)):
+        load(q_nat, q_d, 0, 128)
+        load(s_nat, s_d, 0, 512)
+        load(q_nat, q_d, 128, 512)
+        for lo, hi in ((512, 1024), (1024, 2048), (2048, 3072), (3072, 4096)):
             load(s_nat, s_d, lo, hi)
         for lo, hi in ((512, 2048), (2048, 4096)):
             load(q_nat, q_d, lo, hi)
@@ -88,7 +91,9 @@ def tile_fusionfeature_layer_kernel(tc, query_feature, support_feature, out_0, o
             nc.vector.quantize_mx(out=qcodes[:].bitcast(FP8X4), scales=qscl[:], in_=qgrp[:])
 
         ssum = const.tile([P, 1], F32, name="ssum")
-        ssp = const.tile([P, 32], BF16, name="ssp")
+        ssp = const.tile([P, GN], BF16, name="ssp")
+        sum4 = const.tile([P, 4], F32, name="sum4")
+        sum2 = const.tile([P, 2], F32, name="sum2")
         res1 = const.tile([P, 1], F32, name="res1")
         res2 = const.tile([P, 1], F32, name="res2")
         vsum = const.tile([P, NB], F32, name="vsum")
@@ -97,36 +102,38 @@ def tile_fusionfeature_layer_kernel(tc, query_feature, support_feature, out_0, o
         gate = const.tile([P, NB], F32, name="gate")
         gate1 = const.tile([P, NB], F32, name="gate1")
         o1 = const.tile([P, N], F32, name="o1")
-        nc.vector.memset(ssp[:], 0.0)
+        nc.gpsimd.memset(ssp[:], 0.0)
 
-        gate_split = [
-            lambda: nc.vector.tensor_reduce(out=ssum[:], in_=spart[:], axis=AX.X, op=ALU.add),
-            lambda: nc.vector.tensor_copy(out=ssp[:, 0:1], in_=ssum[:]),
-            lambda: nc.vector.tensor_tensor(out=res1[:], in0=ssum[:], in1=ssp[:, 0:1], op=ALU.subtract),
-            lambda: nc.vector.tensor_copy(out=ssp[:, 1:2], in_=res1[:]),
-            lambda: nc.vector.tensor_tensor(out=res2[:], in0=res1[:], in1=ssp[:, 1:2], op=ALU.subtract),
-            lambda: nc.vector.tensor_copy(out=ssp[:, 2:3], in_=res2[:]),
-        ]
+        def gate_split():
+            nc.gpsimd.tensor_tensor(out=sum4[:], in0=spart[:, 0:4], in1=spart[:, 4:8], op=ALU.add)
+            nc.gpsimd.tensor_tensor(out=sum2[:], in0=sum4[:, 0:2], in1=sum4[:, 2:4], op=ALU.add)
+            nc.gpsimd.tensor_tensor(out=ssum[:], in0=sum2[:, 0:1], in1=sum2[:, 1:2], op=ALU.add)
+            nc.gpsimd.tensor_copy(out=ssp[:, 0:1], in_=ssum[:])
+            nc.gpsimd.tensor_tensor(out=res1[:], in0=ssum[:], in1=ssp[:, 0:1], op=ALU.subtract)
+            nc.gpsimd.tensor_copy(out=ssp[:, 1:2], in_=res1[:])
+            nc.gpsimd.tensor_tensor(out=res2[:], in0=res1[:], in1=ssp[:, 1:2], op=ALU.subtract)
+            nc.gpsimd.tensor_copy(out=ssp[:, 2:3], in_=res2[:])
 
-        def gate_matmuls():
-            for hb in range(2):
-                gp = psum.tile([P, 512], F32, name="gp", tag="adj", bufs=3)
-                for r in range(16):
-                    b = hb * 16 + r
-                    nc.tensor.matmul(out=gp[:, r * 32:(r + 1) * 32], lhsT=qfT[:, b * P:(b + 1) * P], rhs=ssp[:],
-                                     start=True, stop=True)
-                nc.vector.tensor_reduce(out=vsum[:, hb * 16:(hb + 1) * 16],
-                                        in_=gp[:].rearrange("p (r j) -> p r j", j=32)[:, :, 0:3],
-                                        axis=AX.X, op=ALU.add)
+        def gate_matmuls(lo, hi):
+            if lo == 0:
+                st["gp"] = psum.tile([P, NB * GN], F32, name="gp", tag="acc", bufs=1)
+            for b in range(lo, hi):
+                nc.tensor.matmul(out=st["gp"][:, b * GN:(b + 1) * GN], lhsT=qfT[:, b * P:(b + 1) * P], rhs=ssp[:],
+                                 start=True, stop=True)
+
+        def gate_sum():
+            nc.vector.tensor_reduce(out=vsum[:], in_=st["gp"][:].rearrange("p (b j) -> p b j", j=GN),
+                                    axis=AX.X, op=ALU.add)
 
         def gate_exp():
             nc.scalar.activation(out=gexp[:], in_=vsum[:], func=ACTF.Exp, scale=-1.0)
 
-        gate_finish = [
-            lambda: nc.vector.tensor_scalar_add(out=gden[:], in0=gexp[:], scalar1=1.0),
-            lambda: nc.vector.reciprocal(out=gate[:], in_=gden[:]),
-            lambda: nc.vector.tensor_scalar_add(out=gate1[:], in0=gate[:], scalar1=1.0),
-        ]
+        def gate_den():
+            nc.gpsimd.tensor_scalar(out=gden[:], in0=gexp[:], scalar1=1.0, scalar2=1.0, op0=ALU.mult, op1=ALU.add)
+
+        def gate_finish():
+            nc.vector.reciprocal(out=gate[:], in_=gden[:])
+            nc.gpsimd.tensor_scalar(out=gate1[:], in0=gate[:], scalar1=1.0, scalar2=1.0, op0=ALU.mult, op1=ALU.add)
 
         def out1_block(b):
             cols = slice(b * P, (b + 1) * P)
@@ -145,7 +152,8 @@ def tile_fusionfeature_layer_kernel(tc, query_feature, support_feature, out_0, o
                 st["adjs", b] = work.tile([P, N], F32, name="adjs", tag="adjs", bufs=3)
                 st["mx8", b] = work.tile([P, 8], F32, name="mx8", tag="mx8", bufs=3)
             ap = psum.tile([P, 512], F32, name="ap", tag="adj", bufs=3)
-            nc.tensor.matmul(out=ap[:], lhsT=qfT[:, b * P:(b + 1) * P], rhs=sfp[:, j * 512:(j + 1) * 512],
+            rhs = s_nat if b == 0 else sfp
+            nc.tensor.matmul(out=ap[:], lhsT=qfT[:, b * P:(b + 1) * P], rhs=rhs[:, j * 512:(j + 1) * 512],
                              start=True, stop=True)
             nc.vector.tensor_scalar(out=st["adjs", b][:, j * 512:(j + 1) * 512], in0=ap[:], scalar1=1.0,
                                     scalar2=None, op0=ALU.mult, op1=ALU.max,
@@ -191,7 +199,12 @@ def tile_fusionfeature_layer_kernel(tc, query_feature, support_feature, out_0, o
             if r == 0:
                 st["tp", b, k] = psum.tile([P, WBANK], F32, name="tp", tag="tp", bufs=4)
             words = st["e", b][:].bitcast(F32)
-            nc.tensor.transpose(st["tp", b, k][:, r * P:(r + 1) * P], words[:, s * P:(s + 1) * P], ident_w[:])
+            if b == 0:
+                g, u = divmod(s, 2)
+                src = words[:, g * 2 * P + u:(g + 1) * 2 * P:2]
+            else:
+                src = words[:, s * P:(s + 1) * P]
+            nc.tensor.transpose(st["tp", b, k][:, r * P:(r + 1) * P], src, ident_w[:])
 
         def regroup(b, k, engine_copy=nc.scalar.copy):
             if k == 0:
@@ -243,38 +256,43 @@ def tile_fusionfeature_layer_kernel(tc, query_feature, support_feature, out_0, o
                 negmax(1)
             if j >= 1 and i >= 2:
                 fold_max(i, j)
-            if i == 1 and j < len(gate_split):
-                gate_split[j]()
+            if i == 3 and j == 0:
+                gate_sum()
             if i == 3 and j == 1:
                 quantise_qf()
-            if i == 3 and j >= 5:
-                gate_finish[j - 5]()
+            if i == 3 and j == 6:
+                gate_den()
+            if i == 4 and j == 0:
+                gate_finish()
             if 0 <= i - 4 < NB:
-                if j == 1 and i % 2 == 0:
-                    epi_recip(i - 4, i - 2)
-                    epi_weight(i - 4, i - 2, nc.gpsimd)
+                if j == 1 and (i - 4) % 3 == 0:
+                    epi_recip(i - 4, i - 1)
+                    epi_weight(i - 4, i - 1, nc.gpsimd)
                 if j == 6:
                     epi_out(i - 4)
             if j == 3 and 0 <= i - 3 < NB:
                 quant(i - 3)
 
         for i in range(NB):
-            if 0 <= i - 4:
-                out1_block(i - 4)
-            if i == 2:
-                gate_matmuls()
             for j in range(8):
                 adj_evac(i, j)
                 if j == 4 and 0 <= i - 4:
                     mx(i - 4)
                 between(i, j)
-                if i == 0 and j >= 4:
-                    lo = 4 + (j - 4) * 8
-                    qft_blocks(lo, min(lo + 8, NB), nc.scalar.copy)
+                if j == 0 and 0 <= i - 4:
+                    out1_block(i - 4)
+                if i == 0 and j in (4, 6):
+                    lo = 4 + (j - 4) * 4
+                    qft_blocks(lo, lo + 8, nc.scalar.copy)
+                if i == 2:
+                    gate_matmuls(j * 4, (j + 1) * 4)
                 if j == 0 and 0 <= i - 1:
                     expo(i - 1)
-                    if i == 2:
+                    if i == 3:
                         gate_exp()
+                if i == 1 and j in (2, 4):
+                    lo = 20 + (j - 2) * 4
+                    qft_blocks(lo, min(lo + 8, NB), nc.scalar.copy)
                 if 0 <= i - 2 and j % 2 == 1:
                     for s in range(2 * j - 2, 2 * j + 2):
                         transp(i - 2, s)
@@ -283,13 +301,12 @@ def tile_fusionfeature_layer_kernel(tc, query_feature, support_feature, out_0, o
                     regroup(i - 2, j // 2, nc.vector.tensor_copy if j == 1 and i % 5 == 0 else nc.scalar.copy)
             if i == 0:
                 negmax(0)
+                gate_split()
                 for g in range(G):
                     regroup_qf(g)
 
         last = NB - 1
         mx(NB - 4)
-        epi_recip(NB - 4, NB - 2)
-        epi_weight(NB - 4, NB - 2, nc.gpsimd)
         for b in range(NB - 4, NB):
             out1_block(b)
         for k in range(4):

from contextlib import ExitStack

import concourse.mybir as mybir
from concourse.masks import make_identity

F32 = mybir.dt.float32
BF16 = mybir.dt.bfloat16
U32 = mybir.dt.uint32
U8 = mybir.dt.uint8
FP8X4 = mybir.dt.float8_e4m3fn_x4
ALU = mybir.AluOpType
ACTF = mybir.ActivationFunctionType
AX = mybir.AxisListType

P = 128
N = 4096
C = 128
NB = N // P
K_PASS = 512
G = N // K_PASS
BANK = 1024
WBANK = 512
GN = 4
FLOPS = 2 * 2 * N * N * C


def tile_fusionfeature_layer_kernel(tc, query_feature, support_feature, out_0, out_1):
    nc = tc.nc
    q_d = query_feature.rearrange("o c h w -> (o c) (h w)")
    s_d = support_feature.rearrange("o c h w -> (o c) (h w)")
    qmx_d = query_feature.rearrange("o (g a) (b h) w -> (o a b) g (h w)", g=G, a=16, b=8)
    o0_d = out_0.rearrange("o c h w -> (o c) (h w)")
    o1_d = out_1.rearrange("o c h w -> (o c) (h w)")

    with ExitStack() as ctx:
        const = ctx.enter_context(tc.tile_pool(name="const", bufs=1))
        work = ctx.enter_context(tc.tile_pool(name="work", bufs=2))
        psum = ctx.enter_context(tc.psum_pool(name="psum", bufs=1))
        ctx.enter_context(tc.manual_schedule())

        ident = const.tile([P, P], BF16, name="ident")
        make_identity(nc, ident[:])
        ident_w = const.tile([P, P], F32, name="ident_w")
        make_identity(nc, ident_w[:])

        q_nat = const.tile([P, N], BF16, name="q_nat")
        s_nat = const.tile([P, N], BF16, name="s_nat")
        qmx_raw = const.tile([P, G, K_PASS], BF16, name="qmx_raw")

        def load(dst, src, lo, hi):
            nc.sync.dma_start(out=dst[:, lo:hi], in_=src[:, lo:hi])

        load(q_nat, q_d, 0, 128)
        load(s_nat, s_d, 0, 512)
        load(q_nat, q_d, 128, 512)
        for lo, hi in ((512, 1024), (1024, 2048), (2048, 3072), (3072, 4096)):
            load(s_nat, s_d, lo, hi)
        for lo, hi in ((512, 2048), (2048, 4096)):
            load(q_nat, q_d, lo, hi)
        nc.sync.dma_start(out=qmx_raw[:], in_=qmx_d)

        qfT = const.tile([P, N], BF16, name="qfT")

        def qft_blocks(lo, hi, engine_copy):
            tq = psum.tile([P, BANK], BF16, name="tq", tag="tp", bufs=4)
            for b in range(lo, hi):
                nc.tensor.transpose(tq[:, (b - lo) * P:(b - lo + 1) * P], q_nat[:, b * P:(b + 1) * P], ident[:])
            engine_copy(out=qfT[:, lo * P:hi * P], in_=tq[:, 0:(hi - lo) * P])

        qft_blocks(0, 1, nc.vector.tensor_copy)
        qft_blocks(1, 4, nc.vector.tensor_copy)

        sfp = const.tile([P, N], BF16, name="sfp")
        spart = const.tile([P, G], F32, name="spart")
        for g in range(G):
            cols = slice(g * K_PASS, (g + 1) * K_PASS)
            nc.scalar.activation(out=sfp[:, cols].rearrange("c (u p e) -> c u p e", u=2, e=2),
                                 in_=s_nat[:, cols].rearrange("c (p u e) -> c u p e", u=2, e=2),
                                 func=ACTF.Copy, accum_out=spart[:, g:g + 1])

        qgrp = const.tile([P, N], BF16, name="qgrp", align_bytes=64)
        qcodes = const.tile([P, G * C], U32, name="qcodes", align_bytes=64)
        qscl = const.tile([P, G * C], U8, name="qscl", align_bytes=64)

        def regroup_qf(g):
            nc.gpsimd.tensor_scalar(out=qgrp[:, g * K_PASS:(g + 1) * K_PASS].rearrange("p (c t) -> p c t", t=4),
                                    in0=qmx_raw[:, g, :].rearrange("p (t c) -> p c t", t=4),
                                    scalar1=1.0, scalar2=0.0, op0=ALU.mult, op1=ALU.add)

        def quantise_qf():
            nc.vector.quantize_mx(out=qcodes[:].bitcast(FP8X4), scales=qscl[:], in_=qgrp[:])

        ssum = const.tile([P, 1], F32, name="ssum")
        ssp = const.tile([P, GN], BF16, name="ssp")
        sum4 = const.tile([P, 4], F32, name="sum4")
        sum2 = const.tile([P, 2], F32, name="sum2")
        res1 = const.tile([P, 1], F32, name="res1")
        res2 = const.tile([P, 1], F32, name="res2")
        vsum = const.tile([P, NB], F32, name="vsum")
        gexp = const.tile([P, NB], F32, name="gexp")
        gden = const.tile([P, NB], F32, name="gden")
        gate = const.tile([P, NB], F32, name="gate")
        gate1 = const.tile([P, NB], F32, name="gate1")
        o1 = const.tile([P, N], F32, name="o1")
        nc.gpsimd.memset(ssp[:], 0.0)

        def gate_split():
            nc.gpsimd.tensor_tensor(out=sum4[:], in0=spart[:, 0:4], in1=spart[:, 4:8], op=ALU.add)
            nc.gpsimd.tensor_tensor(out=sum2[:], in0=sum4[:, 0:2], in1=sum4[:, 2:4], op=ALU.add)
            nc.gpsimd.tensor_tensor(out=ssum[:], in0=sum2[:, 0:1], in1=sum2[:, 1:2], op=ALU.add)
            nc.gpsimd.tensor_copy(out=ssp[:, 0:1], in_=ssum[:])
            nc.gpsimd.tensor_tensor(out=res1[:], in0=ssum[:], in1=ssp[:, 0:1], op=ALU.subtract)
            nc.gpsimd.tensor_copy(out=ssp[:, 1:2], in_=res1[:])
            nc.gpsimd.tensor_tensor(out=res2[:], in0=res1[:], in1=ssp[:, 1:2], op=ALU.subtract)
            nc.gpsimd.tensor_copy(out=ssp[:, 2:3], in_=res2[:])

        def gate_matmuls(lo, hi):
            if lo == 0:
                st["gp"] = psum.tile([P, NB * GN], F32, name="gp", tag="acc", bufs=1)
            for b in range(lo, hi):
                nc.tensor.matmul(out=st["gp"][:, b * GN:(b + 1) * GN], lhsT=qfT[:, b * P:(b + 1) * P], rhs=ssp[:],
                                 start=True, stop=True)

        def gate_sum():
            nc.vector.tensor_reduce(out=vsum[:], in_=st["gp"][:].rearrange("p (b j) -> p b j", j=GN),
                                    axis=AX.X, op=ALU.add)

        def gate_exp():
            nc.scalar.activation(out=gexp[:], in_=vsum[:], func=ACTF.Exp, scale=-1.0)

        def gate_den():
            nc.gpsimd.tensor_scalar(out=gden[:], in0=gexp[:], scalar1=1.0, scalar2=1.0, op0=ALU.mult, op1=ALU.add)

        def gate_finish():
            nc.vector.reciprocal(out=gate[:], in_=gden[:])
            nc.gpsimd.tensor_scalar(out=gate1[:], in0=gate[:], scalar1=1.0, scalar2=1.0, op0=ALU.mult, op1=ALU.add)

        def out1_block(b):
            cols = slice(b * P, (b + 1) * P)
            nc.gpsimd.tensor_scalar(out=o1[:, cols], in0=s_nat[:, cols], scalar1=gate1[:, b:b + 1], scalar2=0.0,
                                    op0=ALU.mult, op1=ALU.add)
            if b % 8 == 7:
                cc = slice((b - 7) * P, (b + 1) * P)
                nc.sync.dma_start(out=o1_d[:, cc], in_=o1[:, cc])

        o0 = const.tile([P, N], F32, name="o0")
        rs = const.tile([P, NB], F32, name="rs")
        st = {}

        def adj_evac(b, j):
            if j == 0:
                st["adjs", b] = work.tile([P, N], F32, name="adjs", tag="adjs", bufs=3)
                st["mx8", b] = work.tile([P, 8], F32, name="mx8", tag="mx8", bufs=3)
            ap = psum.tile([P, 512], F32, name="ap", tag="adj", bufs=3)
            rhs = s_nat if b == 0 else sfp
            nc.tensor.matmul(out=ap[:], lhsT=qfT[:, b * P:(b + 1) * P], rhs=rhs[:, j * 512:(j + 1) * 512],
                             start=True, stop=True)
            nc.vector.tensor_scalar(out=st["adjs", b][:, j * 512:(j + 1) * 512], in0=ap[:], scalar1=1.0,
                                    scalar2=None, op0=ALU.mult, op1=ALU.max,
                                    accum_out=st["mx8", b][:, j:j + 1])

        def fold_max(b, j):
            mx8 = st["mx8", b]
            if j == 1:
                st["fold", b] = work.tile([P, 8], F32, name="fold", tag="fold", bufs=3)
                st["nm", b] = work.tile([P, 1], F32, name="nm", tag="nm", bufs=3)
            fold = st["fold", b]
            before = mx8[:, 0:1] if j == 1 else fold[:, j - 1:j]
            if j < 7:
                nc.gpsimd.tensor_scalar(out=fold[:, j:j + 1], in0=mx8[:, j:j + 1], scalar1=before, scalar2=None,
                                        op0=ALU.max)
            else:
                nc.gpsimd.tensor_scalar(out=st["nm", b][:], in0=mx8[:, j:j + 1], scalar1=before, scalar2=-1.0,
                                        op0=ALU.max, op1=ALU.mult)

        def negmax(b):
            nm = work.tile([P, 1], F32, name="nm", tag="nm", bufs=3)
            st["nm", b] = nm
            nc.vector.tensor_reduce(out=nm[:], in_=st["mx8", b][:], axis=AX.X, op=ALU.max, negate=True)

        def expo(b):
            e = work.tile([P, N], BF16, name="e", tag="e", bufs=2)
            st["e", b] = e
            nc.scalar.activation(out=e[:], in_=st["adjs", b][:], func=ACTF.Exp, bias=st["nm", b][:],
                                 scale=1.0, accum_out=rs[:, b:b + 1])

        rs_last = const.tile([P, 4], F32, name="rs_last")

        def expo_last(k):
            b = NB - 1
            if k == 0:
                st["e", b] = work.tile([P, N], BF16, name="e", tag="e", bufs=2)
            cols = slice(k * BANK, (k + 1) * BANK)
            nc.scalar.activation(out=st["e", b][:, cols], in_=st["adjs", b][:, cols], func=ACTF.Exp,
                                 bias=st["nm", b][:], scale=1.0, accum_out=rs_last[:, k:k + 1])

        def transp(b, s):
            k, r = divmod(s, 4)
            if r == 0:
                st["tp", b, k] = psum.tile([P, WBANK], F32, name="tp", tag="tp", bufs=4)
            words = st["e", b][:].bitcast(F32)
            if b == 0:
                g, u = divmod(s, 2)
                src = words[:, g * 2 * P + u:(g + 1) * 2 * P:2]
            else:
                src = words[:, s * P:(s + 1) * P]
            nc.tensor.transpose(st["tp", b, k][:, r * P:(r + 1) * P], src, ident_w[:])

        def regroup(b, k, engine_copy=nc.scalar.copy):
            if k == 0:
                st["grp", b] = work.tile([P, N], BF16, name="grp", tag="grp", bufs=2, align_bytes=64)
            words = st["grp", b][:].bitcast(F32)
            dst = words[:, k * WBANK:(k + 1) * WBANK].rearrange("p (g n u) -> p g n u", g=2, u=2)
            src = st["tp", b, k][:].rearrange("p (g u n) -> p g n u", g=2, u=2)
            engine_copy(out=dst, in_=src)

        def quant(b, lo=0, hi=G):
            if lo == 0:
                st["codes", b] = work.tile([P, G * P], U32, name="codes", tag="codes", bufs=2, align_bytes=64)
                st["scl", b] = work.tile([P, G * P], U8, name="scl", tag="scl", bufs=2, align_bytes=64)
            cols = slice(lo * P, hi * P)
            nc.vector.quantize_mx(out=st["codes", b][:, cols].bitcast(FP8X4), scales=st["scl", b][:, cols],
                                  in_=st["grp", b][:, lo * K_PASS:hi * K_PASS])

        def mx(b, lo=0, hi=G):
            if lo == 0:
                tag, bufs = ("acc", 1) if b < NB - 2 else ("adj", 3)
                st["acc", b] = psum.tile([P, C], F32, name="acc", tag=tag, bufs=bufs)
            for g in range(lo, hi):
                cols = slice(g * P, (g + 1) * P)
                nc.tensor.matmul_mx(out=st["acc", b][:], lhsT=st["codes", b][:, cols].bitcast(FP8X4),
                                    lhsT_scale=st["scl", b][:, cols],
                                    rhs=qcodes[:, cols].bitcast(FP8X4), rhs_scale=qscl[:, cols],
                                    start=(g == 0), stop=(g == G - 1))

        rinv = const.tile([P, NB], F32, name="rinv")
        wgt = const.tile([P, NB], F32, name="wgt")

        def epi_recip(lo, hi):
            nc.vector.reciprocal(out=rinv[:, lo:hi], in_=rs[:, lo:hi])

        def epi_weight(lo, hi, engine):
            engine.tensor_tensor(out=wgt[:, lo:hi], in0=rinv[:, lo:hi], in1=gate[:, lo:hi], op=ALU.mult)

        def epi_out(b):
            cols = slice(b * P, (b + 1) * P)
            nc.vector.scalar_tensor_tensor(out=o0[:, cols], in0=st["acc", b][:], scalar=wgt[:, b:b + 1],
                                           in1=q_nat[:, cols], op0=ALU.mult, op1=ALU.add)
            if b % 4 == 3 or b == NB - 2:
                first = b - 2 if b == NB - 2 else (b if b == NB - 1 else b - 3)
                cc = slice(first * P, (b + 1) * P)
                nc.sync.dma_start(out=o0_d[:, cc], in_=o0[:, cc])

        def between(i, j):
            if j == 0 and i == 2:
                negmax(1)
            if j >= 1 and i >= 2:
                fold_max(i, j)
            if i == 3 and j == 0:
                gate_sum()
            if i == 3 and j == 1:
                quantise_qf()
            if i == 3 and j == 6:
                gate_den()
            if i == 4 and j == 0:
                gate_finish()
            if 0 <= i - 4 < NB:
                if j == 1 and (i - 4) % 3 == 0:
                    epi_recip(i - 4, i - 1)
                    epi_weight(i - 4, i - 1, nc.gpsimd)
                if j == 6:
                    epi_out(i - 4)
            if j == 3 and 0 <= i - 3 < NB:
                quant(i - 3)

        for i in range(NB):
            for j in range(8):
                adj_evac(i, j)
                if j == 4 and 0 <= i - 4:
                    mx(i - 4)
                between(i, j)
                if j == 0 and 0 <= i - 4:
                    out1_block(i - 4)
                if i == 0 and j in (4, 6):
                    lo = 4 + (j - 4) * 4
                    qft_blocks(lo, lo + 8, nc.scalar.copy)
                if i == 2:
                    gate_matmuls(j * 4, (j + 1) * 4)
                if j == 0 and 0 <= i - 1:
                    expo(i - 1)
                    if i == 3:
                        gate_exp()
                if i == 1 and j in (2, 4):
                    lo = 20 + (j - 2) * 4
                    qft_blocks(lo, min(lo + 8, NB), nc.scalar.copy)
                if 0 <= i - 2 and j % 2 == 1:
                    for s in range(2 * j - 2, 2 * j + 2):
                        transp(i - 2, s)
                    if i == NB - 1 and j == 7:
                        continue
                    regroup(i - 2, j // 2, nc.vector.tensor_copy if j == 1 and i % 5 == 0 else nc.scalar.copy)
            if i == 0:
                negmax(0)
                gate_split()
                for g in range(G):
                    regroup_qf(g)

        last = NB - 1
        mx(NB - 4)
        for b in range(NB - 4, NB):
            out1_block(b)
        for k in range(4):
            expo_last(k)
        regroup(NB - 3, 3, nc.vector.tensor_copy)
        for s in range(16):
            transp(NB - 2, s)
        regroup(NB - 2, 0, nc.vector.tensor_copy)
        epi_out(NB - 4)
        regroup(NB - 2, 1, nc.vector.tensor_copy)
        quant(NB - 3)
        mx(NB - 3)
        regroup(NB - 2, 2, nc.vector.tensor_copy)
        regroup(NB - 2, 3, nc.vector.tensor_copy)
        epi_out(NB - 3)
        epi_recip(NB - 2, last)
        quant(NB - 2)
        epi_weight(NB - 2, last, nc.vector)
        for s in range(16):
            transp(last, s)
        mx(NB - 2)
        regroup(last, 0)
        for k in range(1, 4):
            regroup(last, k)
        nc.vector.tensor_reduce(out=rs[:, last:NB], in_=rs_last[:], axis=AX.X, op=ALU.add)
        epi_recip(last, NB)
        quant(last, 0, 4)
        mx(last, 0, 4)
        epi_weight(last, NB, nc.vector)
        epi_out(NB - 2)
        quant(last, 4, 6)
        mx(last, 4, 6)
        quant(last, 6, 8)
        mx(last, 6, 8)
        epi_out(last)
